import numpy as np
import ml_dtypes

BF16 = ml_dtypes.bfloat16


def bf(x):
    return np.asarray(x, np.float32).astype(BF16)


def f32(x):
    return np.asarray(x, np.float32)


def f64(x):
    return np.asarray(x).astype(np.float64)


def striped(idx):
    return np.tile(idx.reshape(-1, 16).T, (8, 1))


C, S, N = 256, 2048, 512
PAD = 0
BASE = 10000.0


def pos_table():
    pos = np.arange(1, N + 1, dtype=np.float32)[None, :]
    d = np.arange(C, dtype=np.float32)
    is_sin = (np.arange(C) % 2) == 1
    expo = np.where(is_sin, (d + np.float32(1.0)) / np.float32(C), d / np.float32(C)).astype(np.float32)
    w = np.power(np.float32(1.0 / BASE), expo).astype(np.float32)
    ang = (w[:, None] * pos).astype(np.float32)
    return np.where(is_sin[:, None], np.sin(f64(ang)), np.cos(f64(ang)))


def setup_inputs():
    table = np.random.standard_normal((C, S))
    table[:, PAD] = 0.0
    return {"table": f32(table), "pe": f32(pos_table()), "offs": striped(np.random.permutation(np.tile(np.arange(S), 2))[:N])}


def reference(table, pe, offs):
    idx = offs[:16].T.reshape(-1)
    return f64(table)[:, idx] + f64(pe)

@@ -1,0 +1,26 @@
+import concourse.mybir as mybir
+
+F32 = mybir.dt.float32
+U16 = mybir.dt.uint16
+ADD = mybir.AluOpType.add
+P = 128
+
+
+def tile_positionalembedding_kernel(tc, table, pe, offs, out):
+    nc = tc.nc
+    features, words = table.shape
+    tokens = pe.shape[1]
+
+    with tc.tile_pool(name="held", bufs=1) as held:
+        offsets = held.tile([P, tokens // 16], U16, name="offsets")
+        nc.sync.dma_start(offsets[:], offs)
+
+        for b in range(features // P):
+            rows = slice(b * P, (b + 1) * P)
+            window = held.tile([P, words], F32, name=f"window{b}")
+            place = held.tile([P, tokens], F32, name=f"place{b}")
+            summed = held.tile([P, tokens], F32, name=f"summed{b}")
+            nc.sync.dma_start(window[:], table[rows, :])
+            nc.sync.dma_start(place[:], pe[rows, :])
+            nc.vector.tensor_tensor(summed[:], window[:].indirect(offsets[:]), place[:], ADD)
+            nc.sync.dma_start(out[rows, :], summed[:])

@@ -4,23 +4,35 @@ F32 = mybir.dt.float32
 U16 = mybir.dt.uint16
 ADD = mybir.AluOpType.add
 P = 128
+PIECE = 128
 
 
 def tile_positionalembedding_kernel(tc, table, pe, offs, out):
     nc = tc.nc
     features, words = table.shape
     tokens = pe.shape[1]
+    blocks = features // P
+    pieces = tokens // PIECE
 
     with tc.tile_pool(name="held", bufs=1) as held:
         offsets = held.tile([P, tokens // 16], U16, name="offsets")
         nc.sync.dma_start(offsets[:], offs)
 
-        for b in range(features // P):
+        windows = [held.tile([P, words], F32, name=f"window{b}") for b in range(blocks)]
+        places = [
+            [held.tile([P, PIECE], F32, name=f"place{b}_{k}") for k in range(pieces)]
+            for b in range(blocks)
+        ]
+        for b in range(blocks):
             rows = slice(b * P, (b + 1) * P)
-            window = held.tile([P, words], F32, name=f"window{b}")
-            place = held.tile([P, tokens], F32, name=f"place{b}")
-            summed = held.tile([P, tokens], F32, name=f"summed{b}")
-            nc.sync.dma_start(window[:], table[rows, :])
-            nc.sync.dma_start(place[:], pe[rows, :])
-            nc.vector.tensor_tensor(summed[:], window[:].indirect(offsets[:]), place[:], ADD)
-            nc.sync.dma_start(out[rows, :], summed[:])
+            nc.sync.dma_start(windows[b][:], table[rows, :])
+            for k in range(pieces):
+                nc.sync.dma_start(places[b][k][:], pe[rows, k * PIECE : (k + 1) * PIECE])
+
+        for b in range(blocks):
+            rows = slice(b * P, (b + 1) * P)
+            for k in range(pieces):
+                summed = held.tile([P, PIECE], F32, name=f"summed{b}_{k}")
+                picked = windows[b][:].indirect(offsets[:, k * (PIECE // 16) : (k + 1) * (PIECE // 16)])
+                nc.vector.tensor_tensor(summed[:], picked, places[b][k][:], ADD)
+                nc.sync.dma_start(out[rows, k * PIECE : (k + 1) * PIECE], summed[:])

@@ -4,7 +4,7 @@ F32 = mybir.dt.float32
 U16 = mybir.dt.uint16
 ADD = mybir.AluOpType.add
 P = 128
-PIECE = 128
+PIECE = 256
 
 
 def tile_positionalembedding_kernel(tc, table, pe, offs, out):

@@ -13,6 +13,8 @@ def tile_positionalembedding_kernel(tc, table, pe, offs, out):
     tokens = pe.shape[1]
     blocks = features // P
     pieces = tokens // PIECE
+    queues = (nc.sync, nc.scalar)
+    half = words // len(queues)
 
     with tc.tile_pool(name="held", bufs=1) as held:
         offsets = held.tile([P, tokens // 16], U16, name="offsets")
@@ -25,9 +27,11 @@ def tile_positionalembedding_kernel(tc, table, pe, offs, out):
         ]
         for b in range(blocks):
             rows = slice(b * P, (b + 1) * P)
-            nc.sync.dma_start(windows[b][:], table[rows, :])
+            for h, queue in enumerate(queues):
+                cols = slice(h * half, (h + 1) * half)
+                queue.dma_start(windows[b][:, cols], table[rows, cols])
             for k in range(pieces):
-                nc.sync.dma_start(places[b][k][:], pe[rows, k * PIECE : (k + 1) * PIECE])
+                queues[k % 2].dma_start(places[b][k][:], pe[rows, k * PIECE : (k + 1) * PIECE])
 
         for b in range(blocks):
             rows = slice(b * P, (b + 1) * P)
@@ -35,4 +39,4 @@ def tile_positionalembedding_kernel(tc, table, pe, offs, out):
                 summed = held.tile([P, PIECE], F32, name=f"summed{b}_{k}")
                 picked = windows[b][:].indirect(offsets[:, k * (PIECE // 16) : (k + 1) * (PIECE // 16)])
                 nc.vector.tensor_tensor(summed[:], picked, places[b][k][:], ADD)
-                nc.sync.dma_start(out[rows, k * PIECE : (k + 1) * PIECE], summed[:])
+                queues[k % 2].dma_start(out[rows, k * PIECE : (k + 1) * PIECE], summed[:])

@@ -13,8 +13,6 @@ def tile_positionalembedding_kernel(tc, table, pe, offs, out):
     tokens = pe.shape[1]
     blocks = features // P
     pieces = tokens // PIECE
-    queues = (nc.sync, nc.scalar)
-    half = words // len(queues)
 
     with tc.tile_pool(name="held", bufs=1) as held:
         offsets = held.tile([P, tokens // 16], U16, name="offsets")
@@ -25,13 +23,13 @@ def tile_positionalembedding_kernel(tc, table, pe, offs, out):
             [held.tile([P, PIECE], F32, name=f"place{b}_{k}") for k in range(pieces)]
             for b in range(blocks)
         ]
+
         for b in range(blocks):
             rows = slice(b * P, (b + 1) * P)
-            for h, queue in enumerate(queues):
-                cols = slice(h * half, (h + 1) * half)
-                queue.dma_start(windows[b][:, cols], table[rows, cols])
-            for k in range(pieces):
-                queues[k % 2].dma_start(places[b][k][:], pe[rows, k * PIECE : (k + 1) * PIECE])
+            nc.sync.dma_start(places[b][0][:], pe[rows, 0:PIECE])
+            nc.sync.dma_start(windows[b][:], table[rows, :])
+            for k in range(1, pieces):
+                nc.sync.dma_start(places[b][k][:], pe[rows, k * PIECE : (k + 1) * PIECE])
 
         for b in range(blocks):
             rows = slice(b * P, (b + 1) * P)
@@ -39,4 +37,4 @@ def tile_positionalembedding_kernel(tc, table, pe, offs, out):
                 summed = held.tile([P, PIECE], F32, name=f"summed{b}_{k}")
                 picked = windows[b][:].indirect(offsets[:, k * (PIECE // 16) : (k + 1) * (PIECE // 16)])
                 nc.vector.tensor_tensor(summed[:], picked, places[b][k][:], ADD)
-                queues[k % 2].dma_start(out[rows, k * PIECE : (k + 1) * PIECE], summed[:])
+                nc.sync.dma_start(out[rows, k * PIECE : (k + 1) * PIECE], summed[:])

@@ -4,7 +4,7 @@ F32 = mybir.dt.float32
 U16 = mybir.dt.uint16
 ADD = mybir.AluOpType.add
 P = 128
-PIECE = 256
+EDGE = 128
 
 
 def tile_positionalembedding_kernel(tc, table, pe, offs, out):
@@ -12,29 +12,36 @@ def tile_positionalembedding_kernel(tc, table, pe, offs, out):
     features, words = table.shape
     tokens = pe.shape[1]
     blocks = features // P
-    pieces = tokens // PIECE
+
+    bounds = [[0, tokens // 2, tokens] for b in range(blocks)]
+    bounds[blocks - 1] = [0, EDGE, tokens - EDGE, tokens]
 
     with tc.tile_pool(name="held", bufs=1) as held:
         offsets = held.tile([P, tokens // 16], U16, name="offsets")
         nc.sync.dma_start(offsets[:], offs)
 
-        windows = [held.tile([P, words], F32, name=f"window{b}") for b in range(blocks)]
-        places = [
-            [held.tile([P, PIECE], F32, name=f"place{b}_{k}") for k in range(pieces)]
-            for b in range(blocks)
-        ]
-
+        windows = []
+        early = []
+        late = []
         for b in range(blocks):
             rows = slice(b * P, (b + 1) * P)
-            nc.sync.dma_start(places[b][0][:], pe[rows, 0:PIECE])
+            first = bounds[b][1]
+            windows.append(held.tile([P, words], F32, name=f"window{b}"))
+            early.append(held.tile([P, first], F32, name=f"early{b}"))
+            nc.sync.dma_start(early[b][:], pe[rows, :first])
             nc.sync.dma_start(windows[b][:], table[rows, :])
-            for k in range(1, pieces):
-                nc.sync.dma_start(places[b][k][:], pe[rows, k * PIECE : (k + 1) * PIECE])
+            if first < tokens:
+                late.append(held.tile([P, tokens - first], F32, name=f"late{b}"))
+                nc.sync.dma_start(late[b][:], pe[rows, first:])
+            else:
+                late.append(None)
 
         for b in range(blocks):
             rows = slice(b * P, (b + 1) * P)
-            for k in range(pieces):
-                summed = held.tile([P, PIECE], F32, name=f"summed{b}_{k}")
-                picked = windows[b][:].indirect(offsets[:, k * (PIECE // 16) : (k + 1) * (PIECE // 16)])
-                nc.vector.tensor_tensor(summed[:], picked, places[b][k][:], ADD)
-                nc.sync.dma_start(out[rows, k * PIECE : (k + 1) * PIECE], summed[:])
+            first = bounds[b][1]
+            for lo, hi in zip(bounds[b][:-1], bounds[b][1:]):
+                place = early[b][:] if lo == 0 else late[b][:, lo - first : hi - first]
+                summed = held.tile([P, hi - lo], F32, name=f"summed{b}_{lo}")
+                picked = windows[b][:].indirect(offsets[:, lo // 16 : hi // 16])
+                nc.vector.tensor_tensor(summed[:], picked, place, ADD)
+                nc.sync.dma_start(out[rows, lo:hi], summed[:])

@@ -18,7 +18,6 @@ def tile_positionalembedding_kernel(tc, table, pe, offs, out):
 
     with tc.tile_pool(name="held", bufs=1) as held:
         offsets = held.tile([P, tokens // 16], U16, name="offsets")
-        nc.sync.dma_start(offsets[:], offs)
 
         windows = []
         early = []
@@ -30,6 +29,8 @@ def tile_positionalembedding_kernel(tc, table, pe, offs, out):
             early.append(held.tile([P, first], F32, name=f"early{b}"))
             nc.sync.dma_start(early[b][:], pe[rows, :first])
             nc.sync.dma_start(windows[b][:], table[rows, :])
+            if b == 0:
+                nc.sync.dma_start(offsets[:], offs)
             if first < tokens:
                 late.append(held.tile([P, tokens - first], F32, name=f"late{b}"))
                 nc.sync.dma_start(late[b][:], pe[rows, first:])

@@ -5,6 +5,7 @@ U16 = mybir.dt.uint16
 ADD = mybir.AluOpType.add
 P = 128
 EDGE = 128
+ALIGN = 256
 
 
 def tile_positionalembedding_kernel(tc, table, pe, offs, out):
@@ -25,14 +26,14 @@ def tile_positionalembedding_kernel(tc, table, pe, offs, out):
         for b in range(blocks):
             rows = slice(b * P, (b + 1) * P)
             first = bounds[b][1]
-            windows.append(held.tile([P, words], F32, name=f"window{b}"))
-            early.append(held.tile([P, first], F32, name=f"early{b}"))
+            windows.append(held.tile([P, words], F32, name=f"window{b}", align_bytes=ALIGN))
+            early.append(held.tile([P, first], F32, name=f"early{b}", align_bytes=ALIGN))
             nc.sync.dma_start(early[b][:], pe[rows, :first])
             nc.sync.dma_start(windows[b][:], table[rows, :])
             if b == 0:
                 nc.sync.dma_start(offsets[:], offs)
             if first < tokens:
-                late.append(held.tile([P, tokens - first], F32, name=f"late{b}"))
+                late.append(held.tile([P, tokens - first], F32, name=f"late{b}", align_bytes=ALIGN))
                 nc.sync.dma_start(late[b][:], pe[rows, first:])
             else:
                 late.append(None)
@@ -42,7 +43,7 @@ def tile_positionalembedding_kernel(tc, table, pe, offs, out):
             first = bounds[b][1]
             for lo, hi in zip(bounds[b][:-1], bounds[b][1:]):
                 place = early[b][:] if lo == 0 else late[b][:, lo - first : hi - first]
-                summed = held.tile([P, hi - lo], F32, name=f"summed{b}_{lo}")
+                summed = held.tile([P, hi - lo], F32, name=f"summed{b}_{lo}", align_bytes=ALIGN)
                 picked = windows[b][:].indirect(offsets[:, lo // 16 : hi // 16])
                 nc.vector.tensor_tensor(summed[:], picked, place, ADD)
                 nc.sync.dma_start(out[rows, lo:hi], summed[:])

@@ -5,7 +5,7 @@ U16 = mybir.dt.uint16
 ADD = mybir.AluOpType.add
 P = 128
 EDGE = 128
-ALIGN = 256
+ALIGN = 4096
 
 
 def tile_positionalembedding_kernel(tc, table, pe, offs, out):

@@ -13,37 +13,34 @@ def tile_positionalembedding_kernel(tc, table, pe, offs, out):
     features, words = table.shape
     tokens = pe.shape[1]
     blocks = features // P
+    last = blocks - 1
+
+    windows_in = table.rearrange("(p b) w -> b p w", b=blocks)
+    pe_rows = pe.rearrange("(p b) n -> p (b n)", b=blocks)
+    out_rows = out.rearrange("(p b) n -> p (b n)", b=blocks)
 
     bounds = [[0, tokens // 2, tokens] for b in range(blocks)]
-    bounds[blocks - 1] = [0, EDGE, tokens - EDGE, tokens]
+    bounds[last] = [0, EDGE, tokens - EDGE, tokens]
+    ahead = last * tokens + EDGE
 
     with tc.tile_pool(name="held", bufs=1) as held:
         offsets = held.tile([P, tokens // 16], U16, name="offsets")
+        place = held.tile([P, blocks * tokens], F32, name="place", align_bytes=ALIGN)
+        summed = held.tile([P, blocks * tokens], F32, name="summed", align_bytes=ALIGN)
+        windows = [
+            held.tile([P, words], F32, name=f"window{b}", align_bytes=ALIGN) for b in range(blocks)
+        ]
 
-        windows = []
-        early = []
-        late = []
+        nc.sync.dma_start(place[:, :ahead], pe_rows[:, :ahead])
         for b in range(blocks):
-            rows = slice(b * P, (b + 1) * P)
-            first = bounds[b][1]
-            windows.append(held.tile([P, words], F32, name=f"window{b}", align_bytes=ALIGN))
-            early.append(held.tile([P, first], F32, name=f"early{b}", align_bytes=ALIGN))
-            nc.sync.dma_start(early[b][:], pe[rows, :first])
-            nc.sync.dma_start(windows[b][:], table[rows, :])
+            nc.sync.dma_start(windows[b][:], windows_in[b])
             if b == 0:
                 nc.sync.dma_start(offsets[:], offs)
-            if first < tokens:
-                late.append(held.tile([P, tokens - first], F32, name=f"late{b}", align_bytes=ALIGN))
-                nc.sync.dma_start(late[b][:], pe[rows, first:])
-            else:
-                late.append(None)
+        nc.sync.dma_start(place[:, ahead:], pe_rows[:, ahead:])
 
         for b in range(blocks):
-            rows = slice(b * P, (b + 1) * P)
-            first = bounds[b][1]
             for lo, hi in zip(bounds[b][:-1], bounds[b][1:]):
-                place = early[b][:] if lo == 0 else late[b][:, lo - first : hi - first]
-                summed = held.tile([P, hi - lo], F32, name=f"summed{b}_{lo}", align_bytes=ALIGN)
+                cols = slice(b * tokens + lo, b * tokens + hi)
                 picked = windows[b][:].indirect(offsets[:, lo // 16 : hi // 16])
-                nc.vector.tensor_tensor(summed[:], picked, place, ADD)
-                nc.sync.dma_start(out[rows, lo:hi], summed[:])
+                nc.vector.tensor_tensor(summed[:, cols], picked, place[:, cols], ADD)
+                nc.sync.dma_start(out_rows[:, cols], summed[:, cols])

@@ -19,7 +19,7 @@ def tile_positionalembedding_kernel(tc, table, pe, offs, out):
     pe_rows = pe.rearrange("(p b) n -> p (b n)", b=blocks)
     out_rows = out.rearrange("(p b) n -> p (b n)", b=blocks)
 
-    bounds = [[0, tokens // 2, tokens] for b in range(blocks)]
+    bounds = [[0, tokens] for b in range(blocks)]
     bounds[last] = [0, EDGE, tokens - EDGE, tokens]
     ahead = last * tokens + EDGE
 
@@ -38,9 +38,12 @@ def tile_positionalembedding_kernel(tc, table, pe, offs, out):
                 nc.sync.dma_start(offsets[:], offs)
         nc.sync.dma_start(place[:, ahead:], pe_rows[:, ahead:])
 
+        stored = 0
         for b in range(blocks):
             for lo, hi in zip(bounds[b][:-1], bounds[b][1:]):
                 cols = slice(b * tokens + lo, b * tokens + hi)
                 picked = windows[b][:].indirect(offsets[:, lo // 16 : hi // 16])
                 nc.vector.tensor_tensor(summed[:, cols], picked, place[:, cols], ADD)
-                nc.sync.dma_start(out_rows[:, cols], summed[:, cols])
+                if b == last:
+                    nc.sync.dma_start(out_rows[:, stored : cols.stop], summed[:, stored : cols.stop])
+                    stored = cols.stop

@@ -31,7 +31,7 @@ def tile_positionalembedding_kernel(tc, table, pe, offs, out):
             held.tile([P, words], F32, name=f"window{b}", align_bytes=ALIGN) for b in range(blocks)
         ]
 
-        nc.sync.dma_start(place[:, :ahead], pe_rows[:, :ahead])
+        nc.scalar.dma_start(place[:, :ahead], pe_rows[:, :ahead])
         for b in range(blocks):
             nc.sync.dma_start(windows[b][:], windows_in[b])
             if b == 0:
@@ -45,5 +45,6 @@ def tile_positionalembedding_kernel(tc, table, pe, offs, out):
                 picked = windows[b][:].indirect(offsets[:, lo // 16 : hi // 16])
                 nc.vector.tensor_tensor(summed[:, cols], picked, place[:, cols], ADD)
                 if b == last:
-                    nc.sync.dma_start(out_rows[:, stored : cols.stop], summed[:, stored : cols.stop])
+                    queue = nc.scalar if hi == tokens else nc.sync
+                    queue.dma_start(out_rows[:, stored : cols.stop], summed[:, stored : cols.stop])
                     stored = cols.stop

import concourse.mybir as mybir

F32 = mybir.dt.float32
U16 = mybir.dt.uint16
ADD = mybir.AluOpType.add
P = 128
EDGE = 128
ALIGN = 4096


def tile_positionalembedding_kernel(tc, table, pe, offs, out):
    nc = tc.nc
    features, words = table.shape
    tokens = pe.shape[1]
    blocks = features // P
    last = blocks - 1

    windows_in = table.rearrange("(p b) w -> b p w", b=blocks)
    pe_rows = pe.rearrange("(p b) n -> p (b n)", b=blocks)
    out_rows = out.rearrange("(p b) n -> p (b n)", b=blocks)

    bounds = [[0, tokens] for b in range(blocks)]
    bounds[last] = [0, EDGE, tokens - EDGE, tokens]
    ahead = last * tokens + EDGE

    with tc.tile_pool(name="held", bufs=1) as held:
        offsets = held.tile([P, tokens // 16], U16, name="offsets")
        place = held.tile([P, blocks * tokens], F32, name="place", align_bytes=ALIGN)
        summed = held.tile([P, blocks * tokens], F32, name="summed", align_bytes=ALIGN)
        windows = [
            held.tile([P, words], F32, name=f"window{b}", align_bytes=ALIGN) for b in range(blocks)
        ]

        nc.scalar.dma_start(place[:, :ahead], pe_rows[:, :ahead])
        for b in range(blocks):
            nc.sync.dma_start(windows[b][:], windows_in[b])
            if b == 0:
                nc.sync.dma_start(offsets[:], offs)
        nc.sync.dma_start(place[:, ahead:], pe_rows[:, ahead:])

        stored = 0
        for b in range(blocks):
            for lo, hi in zip(bounds[b][:-1], bounds[b][1:]):
                cols = slice(b * tokens + lo, b * tokens + hi)
                picked = windows[b][:].indirect(offsets[:, lo // 16 : hi // 16])
                nc.vector.tensor_tensor(summed[:, cols], picked, place[:, cols], ADD)
                if b == last:
                    queue = nc.scalar if hi == tokens else nc.sync
                    queue.dma_start(out_rows[:, stored : cols.stop], summed[:, stored : cols.stop])
                    stored = cols.stop
